import numpy as np
import ml_dtypes

BF16 = ml_dtypes.bfloat16


def bf(x):
    return np.asarray(x, np.float32).astype(BF16)


def f32(x):
    return np.asarray(x, np.float32)


def f64(x):
    return np.asarray(x).astype(np.float64)


def striped(idx):
    return np.tile(idx.reshape(-1, 16).T, (8, 1))


C, S, N, P = 512, 512, 256, 4


def setup_inputs():
    t = np.random.standard_normal((C, S))
    return {"x": f32(np.random.standard_normal((C, N, P))), "base": f32(t / np.sqrt((t * t).sum(axis=0, keepdims=True))), "offs": striped(np.random.permutation(S)[:N])}


def reference(x, base, offs):
    idx = offs[:16].T.reshape(-1)
    v = f64(x).sum(axis=2) / P
    r = 1.0 / np.sqrt((v * v).sum(axis=0, keepdims=True))
    res = f64(base).copy()
    res[:, idx] = v * r
    return res

@@ -1,0 +1,49 @@
+import concourse.mybir as mybir
+
+P = 128
+C, S, N, POS = 512, 512, 256, 4
+BLOCKS = C // P
+
+F32, BF16, U16 = mybir.dt.float32, mybir.dt.bfloat16, mybir.dt.uint16
+ADD, MULT = mybir.AluOpType.add, mybir.AluOpType.mult
+SQUARE, SQRT = mybir.ActivationFunctionType.Square, mybir.ActivationFunctionType.Sqrt
+
+FLOPS = 2 * C * N
+
+
+def tile_apkda_kernel(tc, x, base, offs, out):
+    nc = tc.nc
+    with (
+        tc.tile_pool(name="held", bufs=1) as held,
+        tc.psum_pool(name="psum", bufs=1) as psum,
+    ):
+        offsets = held.tile([P, N // 16], U16, name="offsets")
+        nc.sync.dma_start(offsets[:], offs)
+
+        ones = held.tile([P, P], BF16, name="ones")
+        nc.gpsimd.memset(ones[:], 1.0)
+
+        queues = [nc.sync, nc.scalar]
+        maps = [held.tile([P, N, POS], F32, name=f"maps{b}") for b in range(BLOCKS)]
+        windows = [held.tile([P, S], F32, name=f"window{b}") for b in range(BLOCKS)]
+        for b in range(BLOCKS):
+            queues[b % 2].dma_start(maps[b][:], x[b * P : (b + 1) * P])
+        for b in range(BLOCKS):
+            queues[b % 2].dma_start(windows[b][:], base[b * P : (b + 1) * P])
+
+        sums = [held.tile([P, N], F32, name=f"sums{b}") for b in range(BLOCKS)]
+        sumsq = psum.tile([P, N], F32, name="sumsq")
+        for b in range(BLOCKS):
+            nc.vector.tensor_reduce(sums[b][:], maps[b][:], mybir.AxisListType.X, ADD)
+            squares = held.tile([P, N], BF16, name=f"squares{b}")
+            nc.scalar.activation(squares[:], sums[b][:], SQUARE)
+            nc.tensor.matmul(sumsq[:], ones[:], squares[:], start=(b == 0), stop=(b == BLOCKS - 1))
+
+        length = held.tile([P, N], F32, name="length")
+        nc.scalar.activation(length[:], sumsq[:], SQRT)
+        inverse = held.tile([P, N], F32, name="inverse")
+        nc.vector.reciprocal(inverse[:], length[:])
+
+        for b in range(BLOCKS):
+            nc.vector.tensor_tensor(windows[b][:].indirect(offsets[:]), sums[b][:], inverse[:], MULT)
+            queues[b % 2].dma_start(out[b * P : (b + 1) * P], windows[b][:])

@@ -3,10 +3,13 @@ import concourse.mybir as mybir
 P = 128
 C, S, N, POS = 512, 512, 256, 4
 BLOCKS = C // P
+HALVES = 2
+H = N // HALVES
 
 F32, BF16, U16 = mybir.dt.float32, mybir.dt.bfloat16, mybir.dt.uint16
 ADD, MULT = mybir.AluOpType.add, mybir.AluOpType.mult
-SQUARE, SQRT = mybir.ActivationFunctionType.Square, mybir.ActivationFunctionType.Sqrt
+SQUARE = mybir.ActivationFunctionType.Square
+RSQRT = mybir.ActivationFunctionType.Abs_reciprocal_sqrt
 
 FLOPS = 2 * C * N
 
@@ -23,27 +26,32 @@ def tile_apkda_kernel(tc, x, base, offs, out):
         ones = held.tile([P, P], BF16, name="ones")
         nc.gpsimd.memset(ones[:], 1.0)
 
+        warm = held.tile([P, 1], F32, name="warm")
+        nc.scalar.activation(warm[:], ones[:, 0:1], RSQRT)
+
         queues = [nc.sync, nc.scalar]
-        maps = [held.tile([P, N, POS], F32, name=f"maps{b}") for b in range(BLOCKS)]
+        maps = [[held.tile([P, H, POS], F32, name=f"maps{h}{b}") for b in range(BLOCKS)] for h in range(HALVES)]
         windows = [held.tile([P, S], F32, name=f"window{b}") for b in range(BLOCKS)]
-        for b in range(BLOCKS):
-            queues[b % 2].dma_start(maps[b][:], x[b * P : (b + 1) * P])
+        for h in range(HALVES):
+            for b in range(BLOCKS):
+                queues[b % 2].dma_start(maps[h][b][:], x[b * P : (b + 1) * P, h * H : (h + 1) * H])
         for b in range(BLOCKS):
             queues[b % 2].dma_start(windows[b][:], base[b * P : (b + 1) * P])
 
-        sums = [held.tile([P, N], F32, name=f"sums{b}") for b in range(BLOCKS)]
-        sumsq = psum.tile([P, N], F32, name="sumsq")
-        for b in range(BLOCKS):
-            nc.vector.tensor_reduce(sums[b][:], maps[b][:], mybir.AxisListType.X, ADD)
-            squares = held.tile([P, N], BF16, name=f"squares{b}")
-            nc.scalar.activation(squares[:], sums[b][:], SQUARE)
-            nc.tensor.matmul(sumsq[:], ones[:], squares[:], start=(b == 0), stop=(b == BLOCKS - 1))
+        sums = [[held.tile([P, H], F32, name=f"sums{h}{b}") for b in range(BLOCKS)] for h in range(HALVES)]
+        inverse = [held.tile([P, H], F32, name=f"inverse{h}") for h in range(HALVES)]
+        for h in range(HALVES):
+            sumsq = psum.tile([P, H], F32, name=f"sumsq{h}")
+            for b in range(BLOCKS):
+                nc.vector.tensor_reduce(sums[h][b][:], maps[h][b][:], mybir.AxisListType.X, ADD)
+                squares = held.tile([P, H], BF16, name=f"squares{h}{b}")
+                nc.scalar.activation(squares[:], sums[h][b][:], SQUARE)
+                nc.tensor.matmul(sumsq[:], ones[:], squares[:], start=(b == 0), stop=(b == BLOCKS - 1))
+            nc.scalar.activation(inverse[h][:], sumsq[:], RSQRT)
 
-        length = held.tile([P, N], F32, name="length")
-        nc.scalar.activation(length[:], sumsq[:], SQRT)
-        inverse = held.tile([P, N], F32, name="inverse")
-        nc.vector.reciprocal(inverse[:], length[:])
-
+        for h in range(HALVES):
+            piece = offsets[:, h * (H // 16) : (h + 1) * (H // 16)]
+            for b in range(BLOCKS):
+                nc.vector.tensor_tensor(windows[b][:].indirect(piece), sums[h][b][:], inverse[h][:], MULT)
         for b in range(BLOCKS):
-            nc.vector.tensor_tensor(windows[b][:].indirect(offsets[:]), sums[b][:], inverse[:], MULT)
             queues[b % 2].dma_start(out[b * P : (b + 1) * P], windows[b][:])

@@ -43,7 +43,9 @@ def tile_apkda_kernel(tc, x, base, offs, out):
         for h in range(HALVES):
             sumsq = psum.tile([P, H], F32, name=f"sumsq{h}")
             for b in range(BLOCKS):
-                nc.vector.tensor_reduce(sums[h][b][:], maps[h][b][:], mybir.AxisListType.X, ADD)
+                pairs = held.tile([P, H, 2], F32, name=f"pairs{h}{b}")
+                nc.vector.tensor_tensor(pairs[:], maps[h][b][:, :, 0:2], maps[h][b][:, :, 2:4], ADD)
+                nc.vector.tensor_tensor(sums[h][b][:], pairs[:, :, 0], pairs[:, :, 1], ADD)
                 squares = held.tile([P, H], BF16, name=f"squares{h}{b}")
                 nc.scalar.activation(squares[:], sums[h][b][:], SQUARE)
                 nc.tensor.matmul(sumsq[:], ones[:], squares[:], start=(b == 0), stop=(b == BLOCKS - 1))

@@ -26,9 +26,6 @@ def tile_apkda_kernel(tc, x, base, offs, out):
         ones = held.tile([P, P], BF16, name="ones")
         nc.gpsimd.memset(ones[:], 1.0)
 
-        warm = held.tile([P, 1], F32, name="warm")
-        nc.scalar.activation(warm[:], ones[:, 0:1], RSQRT)
-
         queues = [nc.sync, nc.scalar]
         maps = [[held.tile([P, H, POS], F32, name=f"maps{h}{b}") for b in range(BLOCKS)] for h in range(HALVES)]
         windows = [held.tile([P, S], F32, name=f"window{b}") for b in range(BLOCKS)]
@@ -36,7 +33,10 @@ def tile_apkda_kernel(tc, x, base, offs, out):
             for b in range(BLOCKS):
                 queues[b % 2].dma_start(maps[h][b][:], x[b * P : (b + 1) * P, h * H : (h + 1) * H])
         for b in range(BLOCKS):
-            queues[b % 2].dma_start(windows[b][:], base[b * P : (b + 1) * P])
+            nc.sync.dma_start(windows[b][:], base[b * P : (b + 1) * P])
+
+        warm = held.tile([P, 1], F32, name="warm")
+        nc.scalar.activation(warm[:], ones[:, 0:1], RSQRT)
 
         sums = [[held.tile([P, H], F32, name=f"sums{h}{b}") for b in range(BLOCKS)] for h in range(HALVES)]
         inverse = [held.tile([P, H], F32, name=f"inverse{h}") for h in range(HALVES)]

@@ -38,22 +38,27 @@ def tile_apkda_kernel(tc, x, base, offs, out):
         warm = held.tile([P, 1], F32, name="warm")
         nc.scalar.activation(warm[:], ones[:, 0:1], RSQRT)
 
-        sums = [[held.tile([P, H], F32, name=f"sums{h}{b}") for b in range(BLOCKS)] for h in range(HALVES)]
-        inverse = [held.tile([P, H], F32, name=f"inverse{h}") for h in range(HALVES)]
+        sums = [held.tile([P, N], F32, name=f"sums{b}") for b in range(BLOCKS)]
+        inverse = held.tile([P, N], F32, name="inverse")
         for h in range(HALVES):
+            half = slice(h * H, (h + 1) * H)
             sumsq = psum.tile([P, H], F32, name=f"sumsq{h}")
             for b in range(BLOCKS):
                 pairs = held.tile([P, H, 2], F32, name=f"pairs{h}{b}")
                 nc.vector.tensor_tensor(pairs[:], maps[h][b][:, :, 0:2], maps[h][b][:, :, 2:4], ADD)
-                nc.vector.tensor_tensor(sums[h][b][:], pairs[:, :, 0], pairs[:, :, 1], ADD)
+                nc.vector.tensor_tensor(sums[b][:, half], pairs[:, :, 0], pairs[:, :, 1], ADD)
                 squares = held.tile([P, H], BF16, name=f"squares{h}{b}")
-                nc.scalar.activation(squares[:], sums[h][b][:], SQUARE)
+                nc.scalar.activation(squares[:], sums[b][:, half], SQUARE)
                 nc.tensor.matmul(sumsq[:], ones[:], squares[:], start=(b == 0), stop=(b == BLOCKS - 1))
-            nc.scalar.activation(inverse[h][:], sumsq[:], RSQRT)
+            nc.scalar.activation(inverse[:, half], sumsq[:], RSQRT)
 
+        SPLIT = 3
         for h in range(HALVES):
+            half = slice(h * H, (h + 1) * H)
             piece = offsets[:, h * (H // 16) : (h + 1) * (H // 16)]
-            for b in range(BLOCKS):
-                nc.vector.tensor_tensor(windows[b][:].indirect(piece), sums[h][b][:], inverse[h][:], MULT)
+            for b in range(SPLIT):
+                nc.vector.tensor_tensor(windows[b][:].indirect(piece), sums[b][:, half], inverse[:, half], MULT)
+        for b in range(SPLIT, BLOCKS):
+            nc.vector.tensor_tensor(windows[b][:].indirect(offsets[:]), sums[b][:], inverse[:], MULT)
         for b in range(BLOCKS):
             queues[b % 2].dma_start(out[b * P : (b + 1) * P], windows[b][:])

@@ -44,9 +44,10 @@ def tile_apkda_kernel(tc, x, base, offs, out):
             half = slice(h * H, (h + 1) * H)
             sumsq = psum.tile([P, H], F32, name=f"sumsq{h}")
             for b in range(BLOCKS):
-                pairs = held.tile([P, H, 2], F32, name=f"pairs{h}{b}")
-                nc.vector.tensor_tensor(pairs[:], maps[h][b][:, :, 0:2], maps[h][b][:, :, 2:4], ADD)
-                nc.vector.tensor_tensor(sums[b][:, half], pairs[:, :, 0], pairs[:, :, 1], ADD)
+                pairs = held.tile([P, 2, H], F32, name=f"pairs{h}{b}")
+                planes = pairs[:].rearrange("p k n -> p n k")
+                nc.vector.tensor_tensor(planes, maps[h][b][:, :, 0:2], maps[h][b][:, :, 2:4], ADD)
+                nc.vector.tensor_tensor(sums[b][:, half], pairs[:, 0], pairs[:, 1], ADD)
                 squares = held.tile([P, H], BF16, name=f"squares{h}{b}")
                 nc.scalar.activation(squares[:], sums[b][:, half], SQUARE)
                 nc.tensor.matmul(sumsq[:], ones[:], squares[:], start=(b == 0), stop=(b == BLOCKS - 1))

@@ -21,7 +21,6 @@ def tile_apkda_kernel(tc, x, base, offs, out):
         tc.psum_pool(name="psum", bufs=1) as psum,
     ):
         offsets = held.tile([P, N // 16], U16, name="offsets")
-        nc.sync.dma_start(offsets[:], offs)
 
         ones = held.tile([P, P], BF16, name="ones")
         nc.gpsimd.memset(ones[:], 1.0)
@@ -32,6 +31,7 @@ def tile_apkda_kernel(tc, x, base, offs, out):
         for h in range(HALVES):
             for b in range(BLOCKS):
                 queues[b % 2].dma_start(maps[h][b][:], x[b * P : (b + 1) * P, h * H : (h + 1) * H])
+        nc.sync.dma_start(offsets[:], offs)
         for b in range(BLOCKS):
             nc.sync.dma_start(windows[b][:], base[b * P : (b + 1) * P])
 

@@ -8,6 +8,7 @@ H = N // HALVES
 
 F32, BF16, U16 = mybir.dt.float32, mybir.dt.bfloat16, mybir.dt.uint16
 ADD, MULT = mybir.AluOpType.add, mybir.AluOpType.mult
+X = mybir.AxisListType.X
 SQUARE = mybir.ActivationFunctionType.Square
 RSQRT = mybir.ActivationFunctionType.Abs_reciprocal_sqrt
 
@@ -44,10 +45,7 @@ def tile_apkda_kernel(tc, x, base, offs, out):
             half = slice(h * H, (h + 1) * H)
             sumsq = psum.tile([P, H], F32, name=f"sumsq{h}")
             for b in range(BLOCKS):
-                pairs = held.tile([P, 2, H], F32, name=f"pairs{h}{b}")
-                planes = pairs[:].rearrange("p k n -> p n k")
-                nc.vector.tensor_tensor(planes, maps[h][b][:, :, 0:2], maps[h][b][:, :, 2:4], ADD)
-                nc.vector.tensor_tensor(sums[b][:, half], pairs[:, 0], pairs[:, 1], ADD)
+                nc.vector.tensor_reduce(sums[b][:, half], maps[h][b][:], X, ADD)
                 squares = held.tile([P, H], BF16, name=f"squares{h}{b}")
                 nc.scalar.activation(squares[:], sums[b][:, half], SQUARE)
                 nc.tensor.matmul(sumsq[:], ones[:], squares[:], start=(b == 0), stop=(b == BLOCKS - 1))

@@ -29,12 +29,23 @@ def tile_apkda_kernel(tc, x, base, offs, out):
         queues = [nc.sync, nc.scalar]
         maps = [[held.tile([P, H, POS], F32, name=f"maps{h}{b}") for b in range(BLOCKS)] for h in range(HALVES)]
         windows = [held.tile([P, S], F32, name=f"window{b}") for b in range(BLOCKS)]
-        for h in range(HALVES):
-            for b in range(BLOCKS):
-                queues[b % 2].dma_start(maps[h][b][:], x[b * P : (b + 1) * P, h * H : (h + 1) * H])
-        nc.sync.dma_start(offsets[:], offs)
+
+        def load_maps(queue, h, b):
+            queue.dma_start(maps[h][b][:], x[b * P : (b + 1) * P, h * H : (h + 1) * H])
+
+        def load_window(queue, b):
+            queue.dma_start(windows[b][:], base[b * P : (b + 1) * P])
+
         for b in range(BLOCKS):
-            nc.sync.dma_start(windows[b][:], base[b * P : (b + 1) * P])
+            load_maps(queues[b % 2], 0, b)
+        for b in range(BLOCKS - 1):
+            load_maps(queues[b % 2], 1, b)
+        load_window(nc.scalar, 0)
+        nc.sync.dma_start(offsets[:], offs)
+        load_window(nc.sync, 1)
+        load_maps(nc.sync, 1, BLOCKS - 1)
+        for b in range(2, BLOCKS):
+            load_window(nc.sync, b)
 
         warm = held.tile([P, 1], F32, name="warm")
         nc.scalar.activation(warm[:], ones[:, 0:1], RSQRT)

@@ -50,25 +50,34 @@ def tile_apkda_kernel(tc, x, base, offs, out):
         warm = held.tile([P, 1], F32, name="warm")
         nc.scalar.activation(warm[:], ones[:, 0:1], RSQRT)
 
-        sums = [held.tile([P, N], F32, name=f"sums{b}") for b in range(BLOCKS)]
-        inverse = held.tile([P, N], F32, name="inverse")
-        for h in range(HALVES):
-            half = slice(h * H, (h + 1) * H)
-            sumsq = psum.tile([P, H], F32, name=f"sumsq{h}")
-            for b in range(BLOCKS):
-                nc.vector.tensor_reduce(sums[b][:, half], maps[h][b][:], X, ADD)
-                squares = held.tile([P, H], BF16, name=f"squares{h}{b}")
-                nc.scalar.activation(squares[:], sums[b][:, half], SQUARE)
-                nc.tensor.matmul(sumsq[:], ones[:], squares[:], start=(b == 0), stop=(b == BLOCKS - 1))
-            nc.scalar.activation(inverse[:, half], sumsq[:], RSQRT)
+        sums = [[held.tile([P, H], F32, name=f"sums{h}{b}") for b in range(BLOCKS)] for h in range(HALVES)]
+        sumsq = [psum.tile([P, H], F32, name=f"sumsq{h}") for h in range(HALVES)]
+        inverse = [held.tile([P, H], F32, name=f"inverse{h}") for h in range(HALVES)]
 
-        SPLIT = 3
-        for h in range(HALVES):
-            half = slice(h * H, (h + 1) * H)
+        def pool(h, b):
+            nc.vector.tensor_reduce(sums[h][b][:], maps[h][b][:], X, ADD)
+            squares = held.tile([P, H], BF16, name=f"squares{h}{b}")
+            nc.scalar.activation(squares[:], sums[h][b][:], SQUARE)
+            nc.tensor.matmul(sumsq[h][:], ones[:], squares[:], start=(b == 0), stop=(b == BLOCKS - 1))
+
+        def norms(h):
+            nc.scalar.activation(inverse[h][:], sumsq[h][:], RSQRT)
+
+        def place(h, b):
             piece = offsets[:, h * (H // 16) : (h + 1) * (H // 16)]
-            for b in range(SPLIT):
-                nc.vector.tensor_tensor(windows[b][:].indirect(piece), sums[b][:, half], inverse[:, half], MULT)
-        for b in range(SPLIT, BLOCKS):
-            nc.vector.tensor_tensor(windows[b][:].indirect(offsets[:]), sums[b][:], inverse[:], MULT)
+            nc.vector.tensor_tensor(windows[b][:].indirect(piece), sums[h][b][:], inverse[h][:], MULT)
+
         for b in range(BLOCKS):
+            pool(0, b)
+        norms(0)
+        for b in range(BLOCKS - 1):
+            pool(1, b)
+        place(0, 0)
+        place(0, 1)
+        pool(1, BLOCKS - 1)
+        norms(1)
+        place(0, 2)
+        place(0, 3)
+        for b in range(BLOCKS):
+            place(1, b)
             queues[b % 2].dma_start(out[b * P : (b + 1) * P], windows[b][:])

@@ -38,14 +38,15 @@ def tile_apkda_kernel(tc, x, base, offs, out):
 
         for b in range(BLOCKS):
             load_maps(queues[b % 2], 0, b)
-        for b in range(BLOCKS - 1):
-            load_maps(queues[b % 2], 1, b)
-        load_window(nc.scalar, 0)
+        load_maps(nc.sync, 1, 0)
+        load_maps(nc.scalar, 1, 1)
         nc.sync.dma_start(offsets[:], offs)
+        load_maps(nc.scalar, 1, 2)
+        load_window(nc.sync, 0)
         load_window(nc.sync, 1)
-        load_maps(nc.sync, 1, BLOCKS - 1)
-        for b in range(2, BLOCKS):
-            load_window(nc.sync, b)
+        load_maps(nc.sync, 1, 3)
+        load_window(nc.sync, 2)
+        load_window(nc.sync, 3)
 
         warm = held.tile([P, 1], F32, name="warm")
         nc.scalar.activation(warm[:], ones[:, 0:1], RSQRT)

import concourse.mybir as mybir

P = 128
C, S, N, POS = 512, 512, 256, 4
BLOCKS = C // P
HALVES = 2
H = N // HALVES

F32, BF16, U16 = mybir.dt.float32, mybir.dt.bfloat16, mybir.dt.uint16
ADD, MULT = mybir.AluOpType.add, mybir.AluOpType.mult
X = mybir.AxisListType.X
SQUARE = mybir.ActivationFunctionType.Square
RSQRT = mybir.ActivationFunctionType.Abs_reciprocal_sqrt

FLOPS = 2 * C * N


def tile_apkda_kernel(tc, x, base, offs, out):
    nc = tc.nc
    with (
        tc.tile_pool(name="held", bufs=1) as held,
        tc.psum_pool(name="psum", bufs=1) as psum,
    ):
        offsets = held.tile([P, N // 16], U16, name="offsets")

        ones = held.tile([P, P], BF16, name="ones")
        nc.gpsimd.memset(ones[:], 1.0)

        queues = [nc.sync, nc.scalar]
        maps = [[held.tile([P, H, POS], F32, name=f"maps{h}{b}") for b in range(BLOCKS)] for h in range(HALVES)]
        windows = [held.tile([P, S], F32, name=f"window{b}") for b in range(BLOCKS)]

        def load_maps(queue, h, b):
            queue.dma_start(maps[h][b][:], x[b * P : (b + 1) * P, h * H : (h + 1) * H])

        def load_window(queue, b):
            queue.dma_start(windows[b][:], base[b * P : (b + 1) * P])

        for b in range(BLOCKS):
            load_maps(queues[b % 2], 0, b)
        load_maps(nc.sync, 1, 0)
        load_maps(nc.scalar, 1, 1)
        nc.sync.dma_start(offsets[:], offs)
        load_maps(nc.scalar, 1, 2)
        load_window(nc.sync, 0)
        load_window(nc.sync, 1)
        load_maps(nc.sync, 1, 3)
        load_window(nc.sync, 2)
        load_window(nc.sync, 3)

        warm = held.tile([P, 1], F32, name="warm")
        nc.scalar.activation(warm[:], ones[:, 0:1], RSQRT)

        sums = [[held.tile([P, H], F32, name=f"sums{h}{b}") for b in range(BLOCKS)] for h in range(HALVES)]
        sumsq = [psum.tile([P, H], F32, name=f"sumsq{h}") for h in range(HALVES)]
        inverse = [held.tile([P, H], F32, name=f"inverse{h}") for h in range(HALVES)]

        def pool(h, b):
            nc.vector.tensor_reduce(sums[h][b][:], maps[h][b][:], X, ADD)
            squares = held.tile([P, H], BF16, name=f"squares{h}{b}")
            nc.scalar.activation(squares[:], sums[h][b][:], SQUARE)
            nc.tensor.matmul(sumsq[h][:], ones[:], squares[:], start=(b == 0), stop=(b == BLOCKS - 1))

        def norms(h):
            nc.scalar.activation(inverse[h][:], sumsq[h][:], RSQRT)

        def place(h, b):
            piece = offsets[:, h * (H // 16) : (h + 1) * (H // 16)]
            nc.vector.tensor_tensor(windows[b][:].indirect(piece), sums[h][b][:], inverse[h][:], MULT)

        for b in range(BLOCKS):
            pool(0, b)
        norms(0)
        for b in range(BLOCKS - 1):
            pool(1, b)
        place(0, 0)
        place(0, 1)
        pool(1, BLOCKS - 1)
        norms(1)
        place(0, 2)
        place(0, 3)
        for b in range(BLOCKS):
            place(1, b)
            queues[b % 2].dma_start(out[b * P : (b + 1) * P], windows[b][:])
